import numpy as np
import ml_dtypes


def mxq(x, axis, fmt="e4m3"):
    dtype, down = {"e4m3": (ml_dtypes.float8_e4m3fn, 7), "e5m2": (ml_dtypes.float8_e5m2, 14)}[fmt]
    v = np.moveaxis(np.asarray(x, np.float32).astype(ml_dtypes.bfloat16).astype(np.float64), axis, -1)
    blocks = v.reshape(v.shape[:-1] + (-1, 32))
    amax = np.abs(blocks).max(-1, keepdims=True)
    byte = np.maximum(np.where(amax > 0, np.frexp(amax)[1] - 1 + 127, 0) - down, 1)
    scale = np.exp2(byte - 127.0)
    codes = (blocks / scale).astype(np.float32).astype(dtype).astype(np.float64)
    return np.moveaxis((codes * scale).reshape(v.shape), -1, axis)


WIDE = False


def mx_kscale(k):
    if not WIDE:
        return np.ones(k)
    levels = np.array([10, -10, 5, -5, 0])
    if k % 512:
        return np.exp2(np.random.permutation(np.resize(levels, k // 32))).repeat(32)
    a = np.empty((k // 512, 16))
    for p in range(k // 512):
        a[p, :8] = np.random.permutation(np.resize(levels, 8))
        for g in range(8):
            far = levels[np.abs(levels - a[p, g]) >= 10]
            a[p, g + 8] = far[np.random.randint(len(far))]
    return np.exp2(a.ravel()).repeat(32)


BF16 = ml_dtypes.bfloat16


def bf(x):
    return np.asarray(x, np.float32).astype(BF16)


def f64(x):
    return np.asarray(x).astype(np.float64)


E2M1 = np.array([0.0, 0.5, 1.0, 1.5, 2.0, 3.0, 4.0, 6.0, -0.0, -0.5, -1.0, -1.5, -2.0, -3.0, -4.0, -6.0])


def pack_weight(w, fmt):
    k, n = w.shape
    w = f64(bf(w)).reshape(k // 32, 32, n)
    amax = np.abs(w).max(1)
    if fmt == "e4m3":
        byte = np.frexp(amax)[1] - 1 + 127 - 7
    else:
        mant, ex = np.frexp(amax / 6.0)
        byte = np.where(mant > 0.5, ex, ex - 1) + 127
    byte = np.clip(np.where(amax > 0, byte, 1), 1, 254)
    scaled = (w * np.exp2(127.0 - byte)[:, None, :]).reshape(k, n).astype(np.float32)
    by_word = np.ascontiguousarray(scaled.reshape(k // 512, 128, 4, n).transpose(0, 1, 3, 2))
    if fmt == "e4m3":
        words = by_word.astype(ml_dtypes.float8_e4m3fn).view(np.uint8)
    else:
        c = by_word.astype(ml_dtypes.float4_e2m1fn).view(np.uint8) & 0xF
        words = c[..., 0::2] | (c[..., 1::2] << 4)
    return np.ascontiguousarray(words), np.ascontiguousarray(byte.astype(np.uint8).reshape(k // 512, 16, n))


def unpack_weight(words, scales, fmt):
    g, p, n, _ = words.shape
    if fmt == "e4m3":
        vals = np.ascontiguousarray(words).view(ml_dtypes.float8_e4m3fn).astype(np.float64)
    else:
        nib = np.empty((g, p, n, 4), np.uint8)
        nib[..., 0::2] = words & 0xF
        nib[..., 1::2] = words >> 4
        vals = E2M1[nib]
    vals = vals * np.repeat(np.exp2(scales.astype(np.float64) - 127.0), 8, axis=1)[..., None]
    return vals.transpose(0, 1, 3, 2).reshape(g * 512, n)
def pack4(w):
    words, scales = pack_weight(w, "e2m1")
    return words.reshape(words.shape[0], 128, -1), scales


def unpack4(words, scales):
    return unpack_weight(words.reshape(words.shape[0], 128, -1, 2), scales, "e2m1")


B, D_IN, D_OUT = 4096, 1024, 512
EPS = 0.01


def draw0():
    s, t = mx_kscale(D_IN), mx_kscale(D_OUT)
    x = bf(np.random.standard_normal((B, D_IN)) * s)
    W_words, W_scales = pack4((np.random.standard_normal((D_OUT, D_IN)) / np.sqrt(D_IN) / s[None, :] * t[:, None]).T)
    b = bf(np.random.standard_normal(D_OUT) * 0.3 * t)
    g_words, g_scales = pack4((np.random.standard_normal((D_OUT, D_OUT)) / np.sqrt(D_OUT) / t[None, :]).T)
    return {"x": x,
            "W_words": W_words,
            "W_scales": W_scales,
            "b": b,
            "g_words": g_words,
            "g_scales": g_scales,
            "g_bias": bf(np.random.standard_normal(D_OUT) * 0.3)}


def core(x, W_words, W_scales, b, g_words, g_scales, g_bias):
    h = (mxq(f64(x), 1, "e4m3") @ unpack4(W_words, W_scales)) + f64(b)
    c = np.cos((mxq(h, 1, "e4m3") @ unpack4(g_words, g_scales)) + f64(g_bias))
    return np.where(np.abs(c) < EPS, -c, c)


def e4m3fn_bytes(y):
    return np.clip(np.asarray(y, np.float64), -448.0, 448.0).astype(np.float32).astype(ml_dtypes.float8_e4m3fn).view(np.uint8)


def e4m3fn_values(b):
    return np.asarray(b, np.uint8).view(ml_dtypes.float8_e4m3fn).astype(np.float64)


def setup_inputs():
    d = draw0()
    x0 = np.asarray(d['x']).astype(np.float64)
    s = (np.max(np.abs(x0), axis=(0,), keepdims=True) / 448.0).astype(np.float32)
    out = {}
    for k, v in d.items():
        if k == 'x':
            out['x_bytes'] = e4m3fn_bytes(x0 / s.astype(np.float64))
            out['x_scale'] = s
        else:
            out[k] = v
    return out


def reference(x_bytes, x_scale, W_words, W_scales, b, g_words, g_scales, g_bias):
    return core(e4m3fn_values(x_bytes) * x_scale.astype(np.float64), W_words, W_scales, b, g_words, g_scales, g_bias)

@@ -1,0 +1,311 @@
+import math
+from contextlib import ExitStack
+
+import concourse.mybir as mybir
+from concourse.masks import make_identity
+
+F32 = mybir.dt.float32
+BF16 = mybir.dt.bfloat16
+I32 = mybir.dt.int32
+U32 = mybir.dt.uint32
+U8 = mybir.dt.uint8
+E4M3 = mybir.dt.float8_e4m3fn
+E4M3X4 = mybir.dt.float8_e4m3fn_x4
+E2M1X4 = mybir.dt.float4_e2m1fn_x4
+ACT = mybir.ActivationFunctionType
+ALU = mybir.AluOpType
+
+B, D_IN, D_OUT = 4096, 1024, 512
+EPS = 0.01
+FLOPS = 2 * B * D_IN * D_OUT + 2 * B * D_OUT * D_OUT
+
+P = 128
+PACK = 4
+PASSES = D_IN // 512
+GROUPS = (2, 2, 4, 4, 4, 4, 4, 4, 2, 2)
+TWO_PI = 2.0 * math.pi
+RAW_BUFS = 3
+XS_BUFS = 6
+XG_BUFS = 3
+XQ_BUFS = 3
+HG_BUFS = 3
+CT_BUFS = 4
+XT_BUFS = 2
+HP_BUFS = 2
+YP_BUFS = 2
+CP_BUFS = 2
+N_ON_GPSIMD = False
+W_ON_GPSIMD = True
+W_TICK = -1
+WIDE = 2
+UPT = 4
+SPLIT_STORES = 1
+FLIP_ON_VECTOR = (26, 27, 28, 29, 30, 31)
+TICK_ORDER = ["product","turn","gather","quant_x","mm1","hidden","quant_h","mm2","angle","turns","back","turn_back","cosine","square","flip","finish"]
+LAG = {"product":0,"turn":0,"gather":0,"quant_x":0,"mm1":0,"hidden":0,"quant_h":0,"mm2":0,"angle":0,"turns":0,"back":0,"turn_back":3,"cosine":3,"square":3,"flip":3,"finish":3}
+
+
+def tile_onehiddenlayer_t_w4_kernel(tc, x_bytes, x_scale, W_words, W_scales, b, g_words, g_scales, g_bias, out):
+    nc = tc.nc
+    tiles = []
+    starts = []
+    row = 0
+    for gi, n in enumerate(GROUPS):
+        starts.append(row)
+        row += n * P
+        for i in range(n):
+            tiles.append((gi, i))
+
+    with ExitStack() as ctx:
+        const = ctx.enter_context(tc.tile_pool(name="const", bufs=1))
+        sb = ctx.enter_context(tc.tile_pool(name="sb", bufs=2))
+        ps = ctx.enter_context(tc.psum_pool(name="ps", bufs=2))
+
+        raw = {}
+        xs, xt, xg, xq, hp, hg, hq, yp, us, ns, zs, cts, cp, qs, sg, outs = ({} for k in range(16))
+
+        def load(gi, split=False):
+            n = GROUPS[gi]
+            raw[gi] = sb.tile([P, 4, D_IN], U8, tag="raw", bufs=RAW_BUFS, align_bytes=64, name="raw")
+            src = x_bytes[starts[gi] : starts[gi] + n * P, :].rearrange("(p i) k -> p i k", i=n)
+            if split:
+                for i in range(n):
+                    nc.sync.dma_start(out=raw[gi][:, i, :], in_=src[:, i, :])
+            else:
+                nc.sync.dma_start(out=raw[gi][:, :n, :], in_=src)
+
+        scale = const.tile([P, D_IN], F32)
+        w_raw = const.tile([P, PASSES, 2 * D_OUT], U8, align_bytes=64)
+        ws_raw = const.tile([P, PASSES, D_OUT], U8, align_bytes=64)
+        w_codes = const.tile([P, PASSES, 2 * D_OUT], U8, align_bytes=64)
+        w_scales = const.tile([P, PASSES, D_OUT], U8, align_bytes=64)
+        g_codes = const.tile([P, 2 * D_OUT], U8, align_bytes=64)
+        gs = const.tile([P, D_OUT], U8, align_bytes=64)
+        b_bf = const.tile([P, PACK], BF16)
+        b_f = const.tile([P, PACK], F32)
+        gb_rows = const.tile([P, P], BF16)
+        gb_f = const.tile([P, PACK], F32)
+        minus1 = const.tile([P, 1], F32)
+        ident = const.tile([P, P], F32)
+        ident_bf = const.tile([P, P], BF16)
+        dummy = const.tile([P, 1], F32)
+
+        nc.vector.memset(ws_raw[:].rearrange("p g n -> p (g n)").bitcast(I32), 0)
+        nc.vector.memset(gs[:].bitcast(I32), 0)
+        nc.vector.memset(gb_rows[:], 0.0)
+        nc.vector.memset(minus1[:], -1.0)
+        nc.vector.memset(dummy[:], 0.0)
+        nc.scalar.activation(out=dummy[:], in_=dummy[:], func=ACT.Sin)
+        make_identity(nc, ident[:])
+        make_identity(nc, ident_bf[:])
+
+        load(0, split=True)
+        nc.scalar.dma_start(out=scale[:], in_=x_scale.rearrange("o k -> (o k)").partition_broadcast(P))
+        nc.sync.dma_start(out=w_raw[:], in_=W_words.rearrange("g p c -> p g c"))
+        for quad in range(4):
+            nc.sync.dma_start(
+                out=ws_raw[32 * quad : 32 * quad + 4, :, :].bitcast(I32),
+                in_=W_scales[:, 4 * quad : 4 * quad + 4, :].rearrange("g q n -> q g n").bitcast(I32),
+            )
+        nc.scalar.dma_start(out=b_bf[:], in_=b.rearrange("(p t) -> p t", t=PACK))
+        nc.scalar.dma_start(out=gb_rows[0:4, :], in_=g_bias.rearrange("(j m) -> j m", j=4))
+        load(1)
+        nc.sync.dma_start(out=g_codes[:], in_=g_words[0])
+        for quad in range(4):
+            nc.sync.dma_start(
+                out=gs[32 * quad : 32 * quad + 4, :].bitcast(I32),
+                in_=g_scales[0, 4 * quad : 4 * quad + 4, :].bitcast(I32),
+            )
+        if len(GROUPS) > 2:
+            load(2)
+
+        def weights_a():
+            weng = nc.gpsimd if W_ON_GPSIMD else nc.vector
+            for g in range(PASSES):
+                weng.tensor_copy(
+                    out=w_codes[:, g, :].rearrange("p (t m c) -> p m t c", t=PACK, c=2),
+                    in_=w_raw[:, g, :].rearrange("p (m t c) -> p m t c", t=PACK, c=2),
+                )
+            for g in range(PASSES):
+                weng.tensor_copy(
+                    out=w_scales[:, g, :].rearrange("p (t m) -> p m t", t=PACK),
+                    in_=ws_raw[:, g, :].rearrange("p (m t) -> p m t", t=PACK),
+                )
+
+        def biases():
+            nc.vector.tensor_copy(out=b_f[:], in_=b_bf[:])
+            gb_t = ps.tile([P, P], BF16, tag="xt", bufs=XT_BUFS, name="gb_t")
+            nc.tensor.transpose(gb_t[:], gb_rows[:], ident_bf[:])
+            nc.vector.tensor_scalar(out=gb_f[:], in0=gb_t[:, 0:4], scalar1=0.5 * math.pi, scalar2=None, op0=ALU.add)
+
+        def product(t):
+            gi, i = tiles[t]
+            xs[t] = sb.tile([P, D_IN], BF16, tag="xs", bufs=XS_BUFS, align_bytes=64, name="xs")
+            nc.vector.tensor_tensor(out=xs[t][:], in0=raw[gi][:, i, :].bitcast(E4M3), in1=scale[:], op=ALU.mult)
+
+        def turn(t):
+            xt[t] = ps.tile([P, PASSES, 2, P], F32, tag="xt", bufs=XT_BUFS, name="xt")
+            words = xs[t][:].bitcast(F32)
+            for g in range(PASSES):
+                for u in range(2):
+                    nc.tensor.transpose(xt[t][:, g, u, :], words[:, 256 * g + u : 256 * (g + 1) : 2], ident[:])
+
+        def gather(t):
+            xg[t] = sb.tile([P, PASSES, P * PACK], BF16, tag="xg", bufs=XG_BUFS, align_bytes=64, name="xg")
+            nc.scalar.copy(
+                out=xg[t][:].bitcast(F32).rearrange("p g (r u) -> p g r u", u=2),
+                in_=xt[t][:].rearrange("p g u r -> p g r u"),
+            )
+
+        def quant_x(t):
+            codes = sb.tile([P, PASSES * P], U32, tag="xqc", bufs=XQ_BUFS, align_bytes=64, name="xqc")
+            scs = sb.tile([P, PASSES * P], U8, tag="xqs", bufs=XQ_BUFS, align_bytes=64, name="xqs")
+            nc.vector.quantize_mx(out=codes[:].bitcast(E4M3X4), scales=scs[:], in_=xg[t][:].rearrange("p g c -> p (g c)"))
+            xq[t] = (codes, scs)
+
+        def mm1(t):
+            codes, scs = xq[t]
+            hp[t] = ps.tile([P, PACK, P], F32, tag="hp", bufs=HP_BUFS, name="hp")
+            for lane in range(PACK):
+                for g in range(PASSES):
+                    nc.tensor.matmul_mx(
+                        out=hp[t][:, lane, :],
+                        lhsT=w_codes[:, g, 256 * lane : 256 * (lane + 1)].bitcast(E2M1X4),
+                        lhsT_scale=w_scales[:, g, P * lane : P * (lane + 1)],
+                        rhs=codes[:, P * g : P * (g + 1)].bitcast(E4M3X4),
+                        rhs_scale=scs[:, P * g : P * (g + 1)],
+                        start=(g == 0),
+                        stop=(g == PASSES - 1),
+                    )
+
+        def hidden(t):
+            hg[t] = sb.tile([P, P, PACK], BF16, tag="hg", bufs=HG_BUFS, align_bytes=64, name="hg")
+            nc.vector.tensor_tensor(
+                out=hg[t][:],
+                in0=hp[t][:].rearrange("p t r -> p r t"),
+                in1=b_f[:].unsqueeze(1).to_broadcast([P, P, PACK]),
+                op=ALU.add,
+            )
+
+        def quant_h(t):
+            gi, i = tiles[t]
+            if i == 0:
+                hcodes = sb.tile([P, 4 * P], U32, tag="hqc", bufs=2, align_bytes=64, name="hcodes")
+                hscs = sb.tile([P, 4 * P], U8, tag="hqs", bufs=2, align_bytes=64, name="hscs")
+                hq[gi] = (hcodes, hscs)
+            codes, scs = hq[gi]
+            nc.vector.quantize_mx(
+                out=codes[:, P * i : P * (i + 1)].bitcast(E4M3X4),
+                scales=scs[:, P * i : P * (i + 1)],
+                in_=hg[t][:].rearrange("p r t -> p (r t)"),
+            )
+
+        def mm2(gi, j):
+            w = GROUPS[gi] * P
+            codes, scs = hq[gi]
+            yp[gi, j] = ps.tile([P, 512], F32, tag="yp", bufs=YP_BUFS, name="yp")
+            nc.tensor.matmul_mx(
+                out=yp[gi, j][:, :w],
+                lhsT=g_codes[:, 256 * j : 256 * (j + 1)].bitcast(E2M1X4),
+                lhsT_scale=gs[:, P * j : P * (j + 1)],
+                rhs=codes[:, :w].bitcast(E4M3X4),
+                rhs_scale=scs[:, :w],
+                start=True,
+                stop=True,
+            )
+
+        def angle(gi, j):
+            w = GROUPS[gi] * P
+            if j == 0:
+                us[gi] = sb.tile([P, 4, 512], F32, tag="us", bufs=2, name="us")
+                ns[gi] = sb.tile([P, 4, 512], I32, tag="ns", bufs=2, name="ns")
+                zs[gi] = sb.tile([P, 4, 512], F32, tag="zs", bufs=2, name="zs")
+            nc.scalar.activation(out=us[gi][:, j, :w], in_=yp[gi, j][:, :w], func=ACT.Identity, bias=gb_f[:, j : j + 1])
+
+        def turns(gi, h):
+            w = GROUPS[gi] * P
+            js = slice(h * WIDE, (h + 1) * WIDE)
+            eng = nc.gpsimd if N_ON_GPSIMD else nc.vector
+            eng.tensor_scalar(
+                out=ns[gi][:, js, :w], in0=us[gi][:, js, :w], scalar1=1.0 / TWO_PI, scalar2=0.0, op0=ALU.mult, op1=ALU.add
+            )
+
+        def back(gi, h):
+            w = GROUPS[gi] * P
+            js = slice(h * WIDE, (h + 1) * WIDE)
+            nc.vector.tensor_scalar(
+                out=zs[gi][:, js, :w], in0=ns[gi][:, js, :w], scalar1=-TWO_PI, scalar2=None, op0=ALU.mult
+            )
+
+        def turn_back(t):
+            gi, i = tiles[t]
+            cp[t] = ps.tile([P, D_OUT], F32, tag="cp", bufs=CP_BUFS, name="cp")
+            cols = slice(P * i, P * (i + 1))
+            for j in range(4):
+                dst = cp[t][:, P * j : P * (j + 1)]
+                nc.tensor.matmul(dst, us[gi][:, j, cols], ident[:], is_transpose=True, start=True, stop=False)
+                nc.tensor.matmul(dst, zs[gi][:, j, cols], ident[:], is_transpose=True, start=False, stop=True)
+
+        def cosine(t):
+            cts[t] = sb.tile([P, D_OUT], F32, tag="ct", bufs=CT_BUFS, name="ct")
+            nc.scalar.activation(out=cts[t][:], in_=cp[t][:], func=ACT.Sin)
+
+        def square(t):
+            qs[t] = sb.tile([P, D_OUT], F32, tag="qs", bufs=3, name="qs")
+            nc.scalar.activation(out=qs[t][:], in_=cts[t][:], func=ACT.Square)
+
+        def flip(t):
+            sg[t] = sb.tile([P, D_OUT], BF16, tag="sg", bufs=3, name="sg")
+            if t in FLIP_ON_VECTOR:
+                nc.vector.tensor_scalar(out=sg[t][:], in0=qs[t][:], scalar1=EPS * EPS, scalar2=2.0, op0=ALU.is_ge, op1=ALU.mult)
+            else:
+                nc.scalar.activation(out=sg[t][:], in_=qs[t][:], func=ACT.Sign, scale=1.0 / (EPS * EPS), bias=minus1[:])
+
+        def finish(t):
+            gi, i = tiles[t]
+            n = GROUPS[gi]
+            if i == 0:
+                outs[gi] = sb.tile([P, 4, D_OUT], F32, tag="outs", bufs=2, name="outs")
+            if t in FLIP_ON_VECTOR:
+                nc.vector.scalar_tensor_tensor(
+                    out=outs[gi][:, i, :], in0=sg[t][:], scalar=1.0, in1=cts[t][:], op0=ALU.subtract, op1=ALU.mult
+                )
+            else:
+                nc.vector.tensor_tensor(out=outs[gi][:, i, :], in0=cts[t][:], in1=sg[t][:], op=ALU.mult)
+            dst = out[starts[gi] : starts[gi] + n * P, :].rearrange("(p i) c -> p i c", i=n)
+            if gi >= len(GROUPS) - SPLIT_STORES:
+                nc.sync.dma_start(out=dst[:, i, :], in_=outs[gi][:, i, :])
+            elif i == n - 1:
+                nc.sync.dma_start(out=dst, in_=outs[gi][:, :n, :])
+
+
+        nt = len(tiles)
+        last = [max(t for t in range(nt) if tiles[t][0] == gi) for gi in range(len(GROUPS))]
+        tile_stage = {"product": product, "turn": turn, "gather": gather, "quant_x": quant_x, "mm1": mm1, "hidden": hidden,
+                      "quant_h": quant_h, "turn_back": turn_back, "cosine": cosine, "square": square, "flip": flip, "finish": finish}
+        unit_stage = {"mm2": mm2, "angle": angle, "turns": turns, "back": back}
+        if W_ON_GPSIMD:
+            weights_a()
+        if W_TICK < 0:
+            biases()
+        loaded = min(3, len(GROUPS))
+        for tick in range(nt + 60):
+            for name in TICK_ORDER:
+                lag = LAG[name]
+                if name in unit_stage:
+                    width = WIDE if name in ("turns", "back") else 1
+                    for gi in range(len(GROUPS)):
+                        for j in range(0, 4, width):
+                            if tick == last[gi] + lag + j // UPT:
+                                unit_stage[name](gi, j // width)
+                else:
+                    t = tick - lag
+                    if 0 <= t < nt:
+                        tile_stage[name](t)
+                        if name == "product" and tiles[t][1] == 0 and loaded < len(GROUPS) and tiles[t][0] >= 1:
+                            load(loaded)
+                            loaded += 1
+            if tick == W_TICK and not W_ON_GPSIMD:
+                weights_a()
+            if tick == W_TICK:
+                biases()

@@ -22,7 +22,7 @@ FLOPS = 2 * B * D_IN * D_OUT + 2 * B * D_OUT * D_OUT
 P = 128
 PACK = 4
 PASSES = D_IN // 512
-GROUPS = (2, 2, 4, 4, 4, 4, 4, 4, 2, 2)
+GROUPS = (2, 2, 2, 2, 2, 2, 2, 2, 2, 2, 2, 2, 2, 2, 2, 2)
 TWO_PI = 2.0 * math.pi
 RAW_BUFS = 3
 XS_BUFS = 6
@@ -35,14 +35,14 @@ HP_BUFS = 2
 YP_BUFS = 2
 CP_BUFS = 2
 N_ON_GPSIMD = False
-W_ON_GPSIMD = True
-W_TICK = -1
-WIDE = 2
+W_ON_GPSIMD = False
+W_TICK = 0
+WIDE = 4
 UPT = 4
 SPLIT_STORES = 1
 FLIP_ON_VECTOR = (26, 27, 28, 29, 30, 31)
-TICK_ORDER = ["product","turn","gather","quant_x","mm1","hidden","quant_h","mm2","angle","turns","back","turn_back","cosine","square","flip","finish"]
-LAG = {"product":0,"turn":0,"gather":0,"quant_x":0,"mm1":0,"hidden":0,"quant_h":0,"mm2":0,"angle":0,"turns":0,"back":0,"turn_back":3,"cosine":3,"square":3,"flip":3,"finish":3}
+TICK_ORDER = ["product","hidden","turn","square","turn_back","gather","cosine","mm1","back","quant_x","mm2","finish","quant_h","turns","flip","angle"]
+LAG = {"product":0,"turn":1,"gather":1,"quant_x":1,"mm1":2,"hidden":3,"quant_h":3,"mm2":4,"angle":4,"turns":5,"back":6,"turn_back":8,"cosine":8,"square":9,"flip":9,"finish":11}
 
 
 def tile_onehiddenlayer_t_w4_kernel(tc, x_bytes, x_scale, W_words, W_scales, b, g_words, g_scales, g_bias, out):
@@ -60,6 +60,7 @@ def tile_onehiddenlayer_t_w4_kernel(tc, x_bytes, x_scale, W_words, W_scales, b, 
         const = ctx.enter_context(tc.tile_pool(name="const", bufs=1))
         sb = ctx.enter_context(tc.tile_pool(name="sb", bufs=2))
         ps = ctx.enter_context(tc.psum_pool(name="ps", bufs=2))
+        ctx.enter_context(tc.manual_schedule())
 
         raw = {}
         xs, xt, xg, xq, hp, hg, hq, yp, us, ns, zs, cts, cp, qs, sg, outs = ({} for k in range(16))
@@ -123,13 +124,13 @@ def tile_onehiddenlayer_t_w4_kernel(tc, x_bytes, x_scale, W_words, W_scales, b, 
             weng = nc.gpsimd if W_ON_GPSIMD else nc.vector
             for g in range(PASSES):
                 weng.tensor_copy(
-                    out=w_codes[:, g, :].rearrange("p (t m c) -> p m t c", t=PACK, c=2),
-                    in_=w_raw[:, g, :].rearrange("p (m t c) -> p m t c", t=PACK, c=2),
+                    out=w_codes[:, g, :].rearrange("p (t m c) -> p t m c", t=PACK, c=2),
+                    in_=w_raw[:, g, :].rearrange("p (m t c) -> p t m c", t=PACK, c=2),
                 )
             for g in range(PASSES):
                 weng.tensor_copy(
-                    out=w_scales[:, g, :].rearrange("p (t m) -> p m t", t=PACK),
-                    in_=ws_raw[:, g, :].rearrange("p (m t) -> p m t", t=PACK),
+                    out=w_scales[:, g, :].rearrange("p (t m) -> p t m", t=PACK),
+                    in_=ws_raw[:, g, :].rearrange("p (m t) -> p t m", t=PACK),
                 )
 
         def biases():

import math
from contextlib import ExitStack

import concourse.mybir as mybir
from concourse.masks import make_identity

F32 = mybir.dt.float32
BF16 = mybir.dt.bfloat16
I32 = mybir.dt.int32
U32 = mybir.dt.uint32
U8 = mybir.dt.uint8
E4M3 = mybir.dt.float8_e4m3fn
E4M3X4 = mybir.dt.float8_e4m3fn_x4
E2M1X4 = mybir.dt.float4_e2m1fn_x4
ACT = mybir.ActivationFunctionType
ALU = mybir.AluOpType

B, D_IN, D_OUT = 4096, 1024, 512
EPS = 0.01
FLOPS = 2 * B * D_IN * D_OUT + 2 * B * D_OUT * D_OUT

P = 128
PACK = 4
PASSES = D_IN // 512
GROUPS = (2, 2, 2, 2, 2, 2, 2, 2, 2, 2, 2, 2, 2, 2, 2, 2)
TWO_PI = 2.0 * math.pi
RAW_BUFS = 3
XS_BUFS = 6
XG_BUFS = 3
XQ_BUFS = 3
HG_BUFS = 3
CT_BUFS = 4
XT_BUFS = 2
HP_BUFS = 2
YP_BUFS = 2
CP_BUFS = 2
N_ON_GPSIMD = False
W_ON_GPSIMD = False
W_TICK = 0
WIDE = 4
UPT = 4
SPLIT_STORES = 1
FLIP_ON_VECTOR = (26, 27, 28, 29, 30, 31)
TICK_ORDER = ["product","hidden","turn","square","turn_back","gather","cosine","mm1","back","quant_x","mm2","finish","quant_h","turns","flip","angle"]
LAG = {"product":0,"turn":1,"gather":1,"quant_x":1,"mm1":2,"hidden":3,"quant_h":3,"mm2":4,"angle":4,"turns":5,"back":6,"turn_back":8,"cosine":8,"square":9,"flip":9,"finish":11}


def tile_onehiddenlayer_t_w4_kernel(tc, x_bytes, x_scale, W_words, W_scales, b, g_words, g_scales, g_bias, out):
    nc = tc.nc
    tiles = []
    starts = []
    row = 0
    for gi, n in enumerate(GROUPS):
        starts.append(row)
        row += n * P
        for i in range(n):
            tiles.append((gi, i))

    with ExitStack() as ctx:
        const = ctx.enter_context(tc.tile_pool(name="const", bufs=1))
        sb = ctx.enter_context(tc.tile_pool(name="sb", bufs=2))
        ps = ctx.enter_context(tc.psum_pool(name="ps", bufs=2))
        ctx.enter_context(tc.manual_schedule())

        raw = {}
        xs, xt, xg, xq, hp, hg, hq, yp, us, ns, zs, cts, cp, qs, sg, outs = ({} for k in range(16))

        def load(gi, split=False):
            n = GROUPS[gi]
            raw[gi] = sb.tile([P, 4, D_IN], U8, tag="raw", bufs=RAW_BUFS, align_bytes=64, name="raw")
            src = x_bytes[starts[gi] : starts[gi] + n * P, :].rearrange("(p i) k -> p i k", i=n)
            if split:
                for i in range(n):
                    nc.sync.dma_start(out=raw[gi][:, i, :], in_=src[:, i, :])
            else:
                nc.sync.dma_start(out=raw[gi][:, :n, :], in_=src)

        scale = const.tile([P, D_IN], F32)
        w_raw = const.tile([P, PASSES, 2 * D_OUT], U8, align_bytes=64)
        ws_raw = const.tile([P, PASSES, D_OUT], U8, align_bytes=64)
        w_codes = const.tile([P, PASSES, 2 * D_OUT], U8, align_bytes=64)
        w_scales = const.tile([P, PASSES, D_OUT], U8, align_bytes=64)
        g_codes = const.tile([P, 2 * D_OUT], U8, align_bytes=64)
        gs = const.tile([P, D_OUT], U8, align_bytes=64)
        b_bf = const.tile([P, PACK], BF16)
        b_f = const.tile([P, PACK], F32)
        gb_rows = const.tile([P, P], BF16)
        gb_f = const.tile([P, PACK], F32)
        minus1 = const.tile([P, 1], F32)
        ident = const.tile([P, P], F32)
        ident_bf = const.tile([P, P], BF16)
        dummy = const.tile([P, 1], F32)

        nc.vector.memset(ws_raw[:].rearrange("p g n -> p (g n)").bitcast(I32), 0)
        nc.vector.memset(gs[:].bitcast(I32), 0)
        nc.vector.memset(gb_rows[:], 0.0)
        nc.vector.memset(minus1[:], -1.0)
        nc.vector.memset(dummy[:], 0.0)
        nc.scalar.activation(out=dummy[:], in_=dummy[:], func=ACT.Sin)
        make_identity(nc, ident[:])
        make_identity(nc, ident_bf[:])

        load(0, split=True)
        nc.scalar.dma_start(out=scale[:], in_=x_scale.rearrange("o k -> (o k)").partition_broadcast(P))
        nc.sync.dma_start(out=w_raw[:], in_=W_words.rearrange("g p c -> p g c"))
        for quad in range(4):
            nc.sync.dma_start(
                out=ws_raw[32 * quad : 32 * quad + 4, :, :].bitcast(I32),
                in_=W_scales[:, 4 * quad : 4 * quad + 4, :].rearrange("g q n -> q g n").bitcast(I32),
            )
        nc.scalar.dma_start(out=b_bf[:], in_=b.rearrange("(p t) -> p t", t=PACK))
        nc.scalar.dma_start(out=gb_rows[0:4, :], in_=g_bias.rearrange("(j m) -> j m", j=4))
        load(1)
        nc.sync.dma_start(out=g_codes[:], in_=g_words[0])
        for quad in range(4):
            nc.sync.dma_start(
                out=gs[32 * quad : 32 * quad + 4, :].bitcast(I32),
                in_=g_scales[0, 4 * quad : 4 * quad + 4, :].bitcast(I32),
            )
        if len(GROUPS) > 2:
            load(2)

        def weights_a():
            weng = nc.gpsimd if W_ON_GPSIMD else nc.vector
            for g in range(PASSES):
                weng.tensor_copy(
                    out=w_codes[:, g, :].rearrange("p (t m c) -> p t m c", t=PACK, c=2),
                    in_=w_raw[:, g, :].rearrange("p (m t c) -> p t m c", t=PACK, c=2),
                )
            for g in range(PASSES):
                weng.tensor_copy(
                    out=w_scales[:, g, :].rearrange("p (t m) -> p t m", t=PACK),
                    in_=ws_raw[:, g, :].rearrange("p (m t) -> p t m", t=PACK),
                )

        def biases():
            nc.vector.tensor_copy(out=b_f[:], in_=b_bf[:])
            gb_t = ps.tile([P, P], BF16, tag="xt", bufs=XT_BUFS, name="gb_t")
            nc.tensor.transpose(gb_t[:], gb_rows[:], ident_bf[:])
            nc.vector.tensor_scalar(out=gb_f[:], in0=gb_t[:, 0:4], scalar1=0.5 * math.pi, scalar2=None, op0=ALU.add)

        def product(t):
            gi, i = tiles[t]
            xs[t] = sb.tile([P, D_IN], BF16, tag="xs", bufs=XS_BUFS, align_bytes=64, name="xs")
            nc.vector.tensor_tensor(out=xs[t][:], in0=raw[gi][:, i, :].bitcast(E4M3), in1=scale[:], op=ALU.mult)

        def turn(t):
            xt[t] = ps.tile([P, PASSES, 2, P], F32, tag="xt", bufs=XT_BUFS, name="xt")
            words = xs[t][:].bitcast(F32)
            for g in range(PASSES):
                for u in range(2):
                    nc.tensor.transpose(xt[t][:, g, u, :], words[:, 256 * g + u : 256 * (g + 1) : 2], ident[:])

        def gather(t):
            xg[t] = sb.tile([P, PASSES, P * PACK], BF16, tag="xg", bufs=XG_BUFS, align_bytes=64, name="xg")
            nc.scalar.copy(
                out=xg[t][:].bitcast(F32).rearrange("p g (r u) -> p g r u", u=2),
                in_=xt[t][:].rearrange("p g u r -> p g r u"),
            )

        def quant_x(t):
            codes = sb.tile([P, PASSES * P], U32, tag="xqc", bufs=XQ_BUFS, align_bytes=64, name="xqc")
            scs = sb.tile([P, PASSES * P], U8, tag="xqs", bufs=XQ_BUFS, align_bytes=64, name="xqs")
            nc.vector.quantize_mx(out=codes[:].bitcast(E4M3X4), scales=scs[:], in_=xg[t][:].rearrange("p g c -> p (g c)"))
            xq[t] = (codes, scs)

        def mm1(t):
            codes, scs = xq[t]
            hp[t] = ps.tile([P, PACK, P], F32, tag="hp", bufs=HP_BUFS, name="hp")
            for lane in range(PACK):
                for g in range(PASSES):
                    nc.tensor.matmul_mx(
                        out=hp[t][:, lane, :],
                        lhsT=w_codes[:, g, 256 * lane : 256 * (lane + 1)].bitcast(E2M1X4),
                        lhsT_scale=w_scales[:, g, P * lane : P * (lane + 1)],
                        rhs=codes[:, P * g : P * (g + 1)].bitcast(E4M3X4),
                        rhs_scale=scs[:, P * g : P * (g + 1)],
                        start=(g == 0),
                        stop=(g == PASSES - 1),
                    )

        def hidden(t):
            hg[t] = sb.tile([P, P, PACK], BF16, tag="hg", bufs=HG_BUFS, align_bytes=64, name="hg")
            nc.vector.tensor_tensor(
                out=hg[t][:],
                in0=hp[t][:].rearrange("p t r -> p r t"),
                in1=b_f[:].unsqueeze(1).to_broadcast([P, P, PACK]),
                op=ALU.add,
            )

        def quant_h(t):
            gi, i = tiles[t]
            if i == 0:
                hcodes = sb.tile([P, 4 * P], U32, tag="hqc", bufs=2, align_bytes=64, name="hcodes")
                hscs = sb.tile([P, 4 * P], U8, tag="hqs", bufs=2, align_bytes=64, name="hscs")
                hq[gi] = (hcodes, hscs)
            codes, scs = hq[gi]
            nc.vector.quantize_mx(
                out=codes[:, P * i : P * (i + 1)].bitcast(E4M3X4),
                scales=scs[:, P * i : P * (i + 1)],
                in_=hg[t][:].rearrange("p r t -> p (r t)"),
            )

        def mm2(gi, j):
            w = GROUPS[gi] * P
            codes, scs = hq[gi]
            yp[gi, j] = ps.tile([P, 512], F32, tag="yp", bufs=YP_BUFS, name="yp")
            nc.tensor.matmul_mx(
                out=yp[gi, j][:, :w],
                lhsT=g_codes[:, 256 * j : 256 * (j + 1)].bitcast(E2M1X4),
                lhsT_scale=gs[:, P * j : P * (j + 1)],
                rhs=codes[:, :w].bitcast(E4M3X4),
                rhs_scale=scs[:, :w],
                start=True,
                stop=True,
            )

        def angle(gi, j):
            w = GROUPS[gi] * P
            if j == 0:
                us[gi] = sb.tile([P, 4, 512], F32, tag="us", bufs=2, name="us")
                ns[gi] = sb.tile([P, 4, 512], I32, tag="ns", bufs=2, name="ns")
                zs[gi] = sb.tile([P, 4, 512], F32, tag="zs", bufs=2, name="zs")
            nc.scalar.activation(out=us[gi][:, j, :w], in_=yp[gi, j][:, :w], func=ACT.Identity, bias=gb_f[:, j : j + 1])

        def turns(gi, h):
            w = GROUPS[gi] * P
            js = slice(h * WIDE, (h + 1) * WIDE)
            eng = nc.gpsimd if N_ON_GPSIMD else nc.vector
            eng.tensor_scalar(
                out=ns[gi][:, js, :w], in0=us[gi][:, js, :w], scalar1=1.0 / TWO_PI, scalar2=0.0, op0=ALU.mult, op1=ALU.add
            )

        def back(gi, h):
            w = GROUPS[gi] * P
            js = slice(h * WIDE, (h + 1) * WIDE)
            nc.vector.tensor_scalar(
                out=zs[gi][:, js, :w], in0=ns[gi][:, js, :w], scalar1=-TWO_PI, scalar2=None, op0=ALU.mult
            )

        def turn_back(t):
            gi, i = tiles[t]
            cp[t] = ps.tile([P, D_OUT], F32, tag="cp", bufs=CP_BUFS, name="cp")
            cols = slice(P * i, P * (i + 1))
            for j in range(4):
                dst = cp[t][:, P * j : P * (j + 1)]
                nc.tensor.matmul(dst, us[gi][:, j, cols], ident[:], is_transpose=True, start=True, stop=False)
                nc.tensor.matmul(dst, zs[gi][:, j, cols], ident[:], is_transpose=True, start=False, stop=True)

        def cosine(t):
            cts[t] = sb.tile([P, D_OUT], F32, tag="ct", bufs=CT_BUFS, name="ct")
            nc.scalar.activation(out=cts[t][:], in_=cp[t][:], func=ACT.Sin)

        def square(t):
            qs[t] = sb.tile([P, D_OUT], F32, tag="qs", bufs=3, name="qs")
            nc.scalar.activation(out=qs[t][:], in_=cts[t][:], func=ACT.Square)

        def flip(t):
            sg[t] = sb.tile([P, D_OUT], BF16, tag="sg", bufs=3, name="sg")
            if t in FLIP_ON_VECTOR:
                nc.vector.tensor_scalar(out=sg[t][:], in0=qs[t][:], scalar1=EPS * EPS, scalar2=2.0, op0=ALU.is_ge, op1=ALU.mult)
            else:
                nc.scalar.activation(out=sg[t][:], in_=qs[t][:], func=ACT.Sign, scale=1.0 / (EPS * EPS), bias=minus1[:])

        def finish(t):
            gi, i = tiles[t]
            n = GROUPS[gi]
            if i == 0:
                outs[gi] = sb.tile([P, 4, D_OUT], F32, tag="outs", bufs=2, name="outs")
            if t in FLIP_ON_VECTOR:
                nc.vector.scalar_tensor_tensor(
                    out=outs[gi][:, i, :], in0=sg[t][:], scalar=1.0, in1=cts[t][:], op0=ALU.subtract, op1=ALU.mult
                )
            else:
                nc.vector.tensor_tensor(out=outs[gi][:, i, :], in0=cts[t][:], in1=sg[t][:], op=ALU.mult)
            dst = out[starts[gi] : starts[gi] + n * P, :].rearrange("(p i) c -> p i c", i=n)
            if gi >= len(GROUPS) - SPLIT_STORES:
                nc.sync.dma_start(out=dst[:, i, :], in_=outs[gi][:, i, :])
            elif i == n - 1:
                nc.sync.dma_start(out=dst, in_=outs[gi][:, :n, :])


        nt = len(tiles)
        last = [max(t for t in range(nt) if tiles[t][0] == gi) for gi in range(len(GROUPS))]
        tile_stage = {"product": product, "turn": turn, "gather": gather, "quant_x": quant_x, "mm1": mm1, "hidden": hidden,
                      "quant_h": quant_h, "turn_back": turn_back, "cosine": cosine, "square": square, "flip": flip, "finish": finish}
        unit_stage = {"mm2": mm2, "angle": angle, "turns": turns, "back": back}
        if W_ON_GPSIMD:
            weights_a()
        if W_TICK < 0:
            biases()
        loaded = min(3, len(GROUPS))
        for tick in range(nt + 60):
            for name in TICK_ORDER:
                lag = LAG[name]
                if name in unit_stage:
                    width = WIDE if name in ("turns", "back") else 1
                    for gi in range(len(GROUPS)):
                        for j in range(0, 4, width):
                            if tick == last[gi] + lag + j // UPT:
                                unit_stage[name](gi, j // width)
                else:
                    t = tick - lag
                    if 0 <= t < nt:
                        tile_stage[name](t)
                        if name == "product" and tiles[t][1] == 0 and loaded < len(GROUPS) and tiles[t][0] >= 1:
                            load(loaded)
                            loaded += 1
            if tick == W_TICK and not W_ON_GPSIMD:
                weights_a()
            if tick == W_TICK:
                biases()
